import numpy as np
import ml_dtypes

BF16 = ml_dtypes.bfloat16


def bf(x):
    return np.asarray(x, np.float32).astype(BF16)


def f32(x):
    return np.asarray(x, np.float32)


def f64(x):
    return np.asarray(x).astype(np.float64)


def striped(idx):
    return np.tile(idx.reshape(-1, 16).T, (8, 1))


P, F, H, C, S, N = 2, 128, 256, 256, 256, 128


def setup_inputs():
    return {"x": f32(np.random.standard_normal((C, N))),
            "pw": f32(np.eye(P)[:, :, None] + 0.3 * np.random.standard_normal((P, P, N))),
            "lab_bias": f32(0.5 * np.random.standard_normal((C, S))),
            "w1": bf(np.random.standard_normal((F, H)) / np.sqrt(F)),
            "b1": f32(0.1 * np.random.standard_normal((H, 1))),
            "offs": striped(np.random.permutation(S)[:N])}


def reference(x, pw, lab_bias, w1, b1, offs):
    idx = offs[:16].T.reshape(-1)
    xs = f64(x).reshape(P, F, N)
    mix = np.einsum('afj,aej->efj', xs, f64(pw))
    y = f64(lab_bias)[:, idx].reshape(P, F, N) + mix
    h = np.einsum('fk,efj->ekj', f64(w1), y) + f64(b1)[None]
    return h.reshape(P * H, N)

@@ -1,0 +1,70 @@
+import concourse.mybir as mybir
+
+F32 = mybir.dt.float32
+BF16 = mybir.dt.bfloat16
+U16 = mybir.dt.uint16
+MULT = mybir.AluOpType.mult
+ADD = mybir.AluOpType.add
+IDENTITY = mybir.ActivationFunctionType.Identity
+
+NODES = 2
+FEAT = 128
+HIDDEN = 256
+LABS = 256
+SAMPLES = 128
+KBLOCKS = HIDDEN // 128
+
+FLOPS = 2 * NODES * FEAT * HIDDEN * SAMPLES
+
+
+def tile_canonicalgraphadapter_kernel(tc, x, pw, lab_bias, w1, b1, offs, out):
+    nc = tc.nc
+    with (
+        tc.tile_pool(name="held", bufs=1) as held,
+        tc.psum_pool(name="psum", bufs=1) as psum,
+    ):
+        x_sb = held.tile([FEAT, NODES, SAMPLES], F32, name="x_sb")
+        nc.sync.dma_start(x_sb[:], x.rearrange("(a f) j -> f a j", f=FEAT))
+        pw_sb = held.tile([FEAT, NODES * NODES * SAMPLES], F32, name="pw_sb")
+        nc.scalar.dma_start(pw_sb[:], pw.rearrange("a e j -> (a e j)").partition_broadcast(FEAT))
+        offsets = held.tile([128, SAMPLES // 16], U16, name="offsets")
+        nc.sync.dma_start(offsets[:], offs)
+        lab_sb = [held.tile([FEAT, LABS], F32, name=f"lab_sb{e}") for e in range(NODES)]
+        nc.sync.dma_start(lab_sb[0][:], lab_bias[0:FEAT, :])
+        nc.scalar.dma_start(lab_sb[1][:], lab_bias[FEAT : 2 * FEAT, :])
+        w1_sb = held.tile([FEAT, HIDDEN], BF16, name="w1_sb")
+        nc.scalar.dma_start(w1_sb[:], w1)
+        b1_sb = held.tile([128, KBLOCKS], F32, name="b1_sb")
+        with nc.allow_non_contiguous_dma(reason="256 bias values, one to a partition"):
+            nc.gpsimd.dma_start(b1_sb[:], b1.rearrange("(kb p) o -> p (kb o)", p=128))
+
+        prod = held.tile([FEAT, NODES * NODES * SAMPLES], F32, name="prod")
+        nc.vector.tensor_tensor(
+            prod[:].rearrange("f (a e j) -> f a e j", a=NODES, e=NODES),
+            x_sb[:].unsqueeze(2).to_broadcast([FEAT, NODES, NODES, SAMPLES]),
+            pw_sb[:].rearrange("f (a e j) -> f a e j", a=NODES, e=NODES),
+            MULT,
+        )
+        half = NODES * SAMPLES
+        mix = held.tile([FEAT, NODES * SAMPLES], F32, name="mix")
+        nc.vector.tensor_tensor(mix[:], prod[:, 0:half], prod[:, half : 2 * half], ADD)
+
+        y32 = held.tile([FEAT, NODES * SAMPLES], F32, name="y32")
+        for e in range(NODES):
+            cols = slice(e * SAMPLES, (e + 1) * SAMPLES)
+            nc.vector.tensor_tensor(y32[:, cols], lab_sb[e][:].indirect(offsets[:]), mix[:, cols], ADD)
+        y_bf = held.tile([FEAT, NODES * SAMPLES], BF16, name="y_bf")
+        nc.vector.tensor_copy(y_bf[:], y32[:])
+
+        out_blocks = out.rearrange("(e kb p) j -> kb p e j", e=NODES, kb=KBLOCKS)
+        for kb in range(KBLOCKS):
+            acc = psum.tile([128, NODES * SAMPLES], F32, name=f"acc{kb}")
+            nc.tensor.matmul(acc[:], w1_sb[:, kb * 128 : (kb + 1) * 128], y_bf[:], start=True, stop=True)
+            res = held.tile([128, NODES, SAMPLES], F32, name=f"res{kb}")
+            res_flat = res[:].rearrange("p e j -> p (e j)")
+            if kb == 0:
+                nc.vector.tensor_scalar(res_flat, acc[:], b1_sb[:, 0:1], None, ADD)
+                nc.sync.dma_start(out_blocks[0], res[:])
+            else:
+                nc.scalar.activation(res_flat, acc[:], IDENTITY, bias=b1_sb[:, 1:2])
+                nc.scalar.dma_start(out_blocks[1], res[:])

@@ -19,42 +19,43 @@ FLOPS = 2 * NODES * FEAT * HIDDEN * SAMPLES
 
 def tile_canonicalgraphadapter_kernel(tc, x, pw, lab_bias, w1, b1, offs, out):
     nc = tc.nc
+    queues = [nc.sync, nc.scalar]
     with (
         tc.tile_pool(name="held", bufs=1) as held,
         tc.psum_pool(name="psum", bufs=1) as psum,
     ):
-        x_sb = held.tile([FEAT, NODES, SAMPLES], F32, name="x_sb")
-        nc.sync.dma_start(x_sb[:], x.rearrange("(a f) j -> f a j", f=FEAT))
-        pw_sb = held.tile([FEAT, NODES * NODES * SAMPLES], F32, name="pw_sb")
-        nc.scalar.dma_start(pw_sb[:], pw.rearrange("a e j -> (a e j)").partition_broadcast(FEAT))
+        x_sb = [held.tile([FEAT, SAMPLES], F32, name=f"x_sb{a}") for a in range(NODES)]
+        pw_sb = [held.tile([FEAT, NODES * SAMPLES], F32, name=f"pw_sb{a}") for a in range(NODES)]
+        for a in range(NODES):
+            queues[a].dma_start(x_sb[a][:], x[a * FEAT : (a + 1) * FEAT, :])
+            queues[1 - a].dma_start(pw_sb[a][:], pw[a].rearrange("e j -> (e j)").partition_broadcast(FEAT))
         offsets = held.tile([128, SAMPLES // 16], U16, name="offsets")
         nc.sync.dma_start(offsets[:], offs)
         lab_sb = [held.tile([FEAT, LABS], F32, name=f"lab_sb{e}") for e in range(NODES)]
-        nc.sync.dma_start(lab_sb[0][:], lab_bias[0:FEAT, :])
-        nc.scalar.dma_start(lab_sb[1][:], lab_bias[FEAT : 2 * FEAT, :])
+        for e in range(NODES):
+            queues[e].dma_start(lab_sb[e][:], lab_bias[e * FEAT : (e + 1) * FEAT, :])
         w1_sb = held.tile([FEAT, HIDDEN], BF16, name="w1_sb")
         nc.scalar.dma_start(w1_sb[:], w1)
         b1_sb = held.tile([128, KBLOCKS], F32, name="b1_sb")
         with nc.allow_non_contiguous_dma(reason="256 bias values, one to a partition"):
-            nc.gpsimd.dma_start(b1_sb[:], b1.rearrange("(kb p) o -> p (kb o)", p=128))
+            nc.sync.dma_start(b1_sb[:], b1.rearrange("(kb p) o -> p (kb o)", p=128))
 
-        prod = held.tile([FEAT, NODES * NODES * SAMPLES], F32, name="prod")
-        nc.vector.tensor_tensor(
-            prod[:].rearrange("f (a e j) -> f a e j", a=NODES, e=NODES),
-            x_sb[:].unsqueeze(2).to_broadcast([FEAT, NODES, NODES, SAMPLES]),
-            pw_sb[:].rearrange("f (a e j) -> f a e j", a=NODES, e=NODES),
-            MULT,
-        )
-        half = NODES * SAMPLES
-        mix = held.tile([FEAT, NODES * SAMPLES], F32, name="mix")
-        nc.vector.tensor_tensor(mix[:], prod[:, 0:half], prod[:, half : 2 * half], ADD)
+        prod = [held.tile([FEAT, NODES, SAMPLES], F32, name=f"prod{a}") for a in range(NODES)]
+        for a in range(NODES):
+            nc.vector.tensor_tensor(
+                prod[a][:],
+                x_sb[a][:].unsqueeze(1).to_broadcast([FEAT, NODES, SAMPLES]),
+                pw_sb[a][:].rearrange("f (e j) -> f e j", e=NODES),
+                MULT,
+            )
+        mix = held.tile([FEAT, NODES, SAMPLES], F32, name="mix")
+        nc.vector.tensor_tensor(mix[:], prod[0][:], prod[1][:], ADD)
 
-        y32 = held.tile([FEAT, NODES * SAMPLES], F32, name="y32")
+        y32 = held.tile([FEAT, NODES, SAMPLES], F32, name="y32")
         for e in range(NODES):
-            cols = slice(e * SAMPLES, (e + 1) * SAMPLES)
-            nc.vector.tensor_tensor(y32[:, cols], lab_sb[e][:].indirect(offsets[:]), mix[:, cols], ADD)
+            nc.vector.tensor_tensor(y32[:, e, :], lab_sb[e][:].indirect(offsets[:]), mix[:, e, :], ADD)
         y_bf = held.tile([FEAT, NODES * SAMPLES], BF16, name="y_bf")
-        nc.vector.tensor_copy(y_bf[:], y32[:])
+        nc.vector.tensor_copy(y_bf[:], y32[:].rearrange("f e j -> f (e j)"))
 
         out_blocks = out.rearrange("(e kb p) j -> kb p e j", e=NODES, kb=KBLOCKS)
         for kb in range(KBLOCKS):
@@ -64,7 +65,6 @@ def tile_canonicalgraphadapter_kernel(tc, x, pw, lab_bias, w1, b1, offs, out):
             res_flat = res[:].rearrange("p e j -> p (e j)")
             if kb == 0:
                 nc.vector.tensor_scalar(res_flat, acc[:], b1_sb[:, 0:1], None, ADD)
-                nc.sync.dma_start(out_blocks[0], res[:])
             else:
                 nc.scalar.activation(res_flat, acc[:], IDENTITY, bias=b1_sb[:, 1:2])
-                nc.scalar.dma_start(out_blocks[1], res[:])
+            queues[kb].dma_start(out_blocks[kb], res[:])

@@ -19,43 +19,46 @@ FLOPS = 2 * NODES * FEAT * HIDDEN * SAMPLES
 
 def tile_canonicalgraphadapter_kernel(tc, x, pw, lab_bias, w1, b1, offs, out):
     nc = tc.nc
-    queues = [nc.sync, nc.scalar]
     with (
         tc.tile_pool(name="held", bufs=1) as held,
         tc.psum_pool(name="psum", bufs=1) as psum,
     ):
-        x_sb = [held.tile([FEAT, SAMPLES], F32, name=f"x_sb{a}") for a in range(NODES)]
-        pw_sb = [held.tile([FEAT, NODES * SAMPLES], F32, name=f"pw_sb{a}") for a in range(NODES)]
-        for a in range(NODES):
-            queues[a].dma_start(x_sb[a][:], x[a * FEAT : (a + 1) * FEAT, :])
-            queues[1 - a].dma_start(pw_sb[a][:], pw[a].rearrange("e j -> (e j)").partition_broadcast(FEAT))
+        x_sb = held.tile([FEAT, NODES, SAMPLES], F32, name="x_sb")
+        nc.sync.dma_start(x_sb[:], x.rearrange("(a f) j -> f a j", f=FEAT))
+        pw_sb = held.tile([FEAT, NODES * NODES * SAMPLES], F32, name="pw_sb")
+        nc.scalar.dma_start(pw_sb[:], pw.rearrange("a e j -> (a e j)").partition_broadcast(FEAT))
         offsets = held.tile([128, SAMPLES // 16], U16, name="offsets")
         nc.sync.dma_start(offsets[:], offs)
         lab_sb = [held.tile([FEAT, LABS], F32, name=f"lab_sb{e}") for e in range(NODES)]
-        for e in range(NODES):
-            queues[e].dma_start(lab_sb[e][:], lab_bias[e * FEAT : (e + 1) * FEAT, :])
+        nc.sync.dma_start(lab_sb[0][:], lab_bias[0:FEAT, :])
+        nc.scalar.dma_start(lab_sb[1][:], lab_bias[FEAT : 2 * FEAT, :])
         w1_sb = held.tile([FEAT, HIDDEN], BF16, name="w1_sb")
         nc.scalar.dma_start(w1_sb[:], w1)
         b1_sb = held.tile([128, KBLOCKS], F32, name="b1_sb")
         with nc.allow_non_contiguous_dma(reason="256 bias values, one to a partition"):
-            nc.sync.dma_start(b1_sb[:], b1.rearrange("(kb p) o -> p (kb o)", p=128))
+            nc.gpsimd.dma_start(b1_sb[:], b1.rearrange("(kb p) o -> p (kb o)", p=128))
 
-        prod = [held.tile([FEAT, NODES, SAMPLES], F32, name=f"prod{a}") for a in range(NODES)]
-        for a in range(NODES):
-            nc.vector.tensor_tensor(
-                prod[a][:],
-                x_sb[a][:].unsqueeze(1).to_broadcast([FEAT, NODES, SAMPLES]),
-                pw_sb[a][:].rearrange("f (e j) -> f e j", e=NODES),
-                MULT,
-            )
-        mix = held.tile([FEAT, NODES, SAMPLES], F32, name="mix")
-        nc.vector.tensor_tensor(mix[:], prod[0][:], prod[1][:], ADD)
+        warm = held.tile([128, 2], F32, name="warm")
+        nc.vector.memset(warm[:, 0:1], 0.0)
+        nc.scalar.activation(warm[:, 1:2], warm[:, 0:1], IDENTITY)
 
-        y32 = held.tile([FEAT, NODES, SAMPLES], F32, name="y32")
+        prod = held.tile([FEAT, NODES * NODES * SAMPLES], F32, name="prod")
+        nc.vector.tensor_tensor(
+            prod[:].rearrange("f (a e j) -> f a e j", a=NODES, e=NODES),
+            x_sb[:].unsqueeze(2).to_broadcast([FEAT, NODES, NODES, SAMPLES]),
+            pw_sb[:].rearrange("f (a e j) -> f a e j", a=NODES, e=NODES),
+            MULT,
+        )
+        half = NODES * SAMPLES
+        mix = held.tile([FEAT, NODES * SAMPLES], F32, name="mix")
+        nc.vector.tensor_tensor(mix[:], prod[:, 0:half], prod[:, half : 2 * half], ADD)
+
+        y32 = held.tile([FEAT, NODES * SAMPLES], F32, name="y32")
         for e in range(NODES):
-            nc.vector.tensor_tensor(y32[:, e, :], lab_sb[e][:].indirect(offsets[:]), mix[:, e, :], ADD)
+            cols = slice(e * SAMPLES, (e + 1) * SAMPLES)
+            nc.vector.tensor_tensor(y32[:, cols], lab_sb[e][:].indirect(offsets[:]), mix[:, cols], ADD)
         y_bf = held.tile([FEAT, NODES * SAMPLES], BF16, name="y_bf")
-        nc.vector.tensor_copy(y_bf[:], y32[:].rearrange("f e j -> f (e j)"))
+        nc.vector.tensor_copy(y_bf[:], y32[:])
 
         out_blocks = out.rearrange("(e kb p) j -> kb p e j", e=NODES, kb=KBLOCKS)
         for kb in range(KBLOCKS):
@@ -65,6 +68,7 @@ def tile_canonicalgraphadapter_kernel(tc, x, pw, lab_bias, w1, b1, offs, out):
             res_flat = res[:].rearrange("p e j -> p (e j)")
             if kb == 0:
                 nc.vector.tensor_scalar(res_flat, acc[:], b1_sb[:, 0:1], None, ADD)
+                nc.sync.dma_start(out_blocks[0], res[:])
             else:
                 nc.scalar.activation(res_flat, acc[:], IDENTITY, bias=b1_sb[:, 1:2])
-            queues[kb].dma_start(out_blocks[kb], res[:])
+                nc.scalar.dma_start(out_blocks[1], res[:])

@@ -19,19 +19,21 @@ FLOPS = 2 * NODES * FEAT * HIDDEN * SAMPLES
 
 def tile_canonicalgraphadapter_kernel(tc, x, pw, lab_bias, w1, b1, offs, out):
     nc = tc.nc
+    queues = [nc.sync, nc.scalar]
     with (
         tc.tile_pool(name="held", bufs=1) as held,
         tc.psum_pool(name="psum", bufs=1) as psum,
     ):
-        x_sb = held.tile([FEAT, NODES, SAMPLES], F32, name="x_sb")
-        nc.sync.dma_start(x_sb[:], x.rearrange("(a f) j -> f a j", f=FEAT))
-        pw_sb = held.tile([FEAT, NODES * NODES * SAMPLES], F32, name="pw_sb")
-        nc.scalar.dma_start(pw_sb[:], pw.rearrange("a e j -> (a e j)").partition_broadcast(FEAT))
+        x_sb = [held.tile([FEAT, SAMPLES], F32, name=f"x_sb{a}") for a in range(NODES)]
+        pw_sb = [held.tile([FEAT, NODES * SAMPLES], F32, name=f"pw_sb{a}") for a in range(NODES)]
+        for a in range(NODES):
+            queues[a].dma_start(x_sb[a][:], x[a * FEAT : (a + 1) * FEAT, :])
+            queues[1 - a].dma_start(pw_sb[a][:], pw[a].rearrange("e j -> (e j)").partition_broadcast(FEAT))
         offsets = held.tile([128, SAMPLES // 16], U16, name="offsets")
         nc.sync.dma_start(offsets[:], offs)
         lab_sb = [held.tile([FEAT, LABS], F32, name=f"lab_sb{e}") for e in range(NODES)]
-        nc.sync.dma_start(lab_sb[0][:], lab_bias[0:FEAT, :])
-        nc.scalar.dma_start(lab_sb[1][:], lab_bias[FEAT : 2 * FEAT, :])
+        for e in range(NODES):
+            queues[e].dma_start(lab_sb[e][:], lab_bias[e * FEAT : (e + 1) * FEAT, :])
         w1_sb = held.tile([FEAT, HIDDEN], BF16, name="w1_sb")
         nc.scalar.dma_start(w1_sb[:], w1)
         b1_sb = held.tile([128, KBLOCKS], F32, name="b1_sb")
@@ -42,23 +44,22 @@ def tile_canonicalgraphadapter_kernel(tc, x, pw, lab_bias, w1, b1, offs, out):
         nc.vector.memset(warm[:, 0:1], 0.0)
         nc.scalar.activation(warm[:, 1:2], warm[:, 0:1], IDENTITY)
 
-        prod = held.tile([FEAT, NODES * NODES * SAMPLES], F32, name="prod")
-        nc.vector.tensor_tensor(
-            prod[:].rearrange("f (a e j) -> f a e j", a=NODES, e=NODES),
-            x_sb[:].unsqueeze(2).to_broadcast([FEAT, NODES, NODES, SAMPLES]),
-            pw_sb[:].rearrange("f (a e j) -> f a e j", a=NODES, e=NODES),
-            MULT,
-        )
-        half = NODES * SAMPLES
-        mix = held.tile([FEAT, NODES * SAMPLES], F32, name="mix")
-        nc.vector.tensor_tensor(mix[:], prod[:, 0:half], prod[:, half : 2 * half], ADD)
+        prod = [held.tile([FEAT, NODES, SAMPLES], F32, name=f"prod{a}") for a in range(NODES)]
+        for a in range(NODES):
+            nc.vector.tensor_tensor(
+                prod[a][:],
+                x_sb[a][:].unsqueeze(1).to_broadcast([FEAT, NODES, SAMPLES]),
+                pw_sb[a][:].rearrange("f (e j) -> f e j", e=NODES),
+                MULT,
+            )
+        mix = held.tile([FEAT, NODES, SAMPLES], F32, name="mix")
+        nc.vector.tensor_tensor(mix[:], prod[0][:], prod[1][:], ADD)
 
-        y32 = held.tile([FEAT, NODES * SAMPLES], F32, name="y32")
+        y32 = held.tile([FEAT, NODES, SAMPLES], F32, name="y32")
         for e in range(NODES):
-            cols = slice(e * SAMPLES, (e + 1) * SAMPLES)
-            nc.vector.tensor_tensor(y32[:, cols], lab_sb[e][:].indirect(offsets[:]), mix[:, cols], ADD)
+            nc.vector.tensor_tensor(y32[:, e, :], lab_sb[e][:].indirect(offsets[:]), mix[:, e, :], ADD)
         y_bf = held.tile([FEAT, NODES * SAMPLES], BF16, name="y_bf")
-        nc.vector.tensor_copy(y_bf[:], y32[:])
+        nc.vector.tensor_copy(y_bf[:], y32[:].rearrange("f e j -> f (e j)"))
 
         out_blocks = out.rearrange("(e kb p) j -> kb p e j", e=NODES, kb=KBLOCKS)
         for kb in range(KBLOCKS):
@@ -68,7 +69,6 @@ def tile_canonicalgraphadapter_kernel(tc, x, pw, lab_bias, w1, b1, offs, out):
             res_flat = res[:].rearrange("p e j -> p (e j)")
             if kb == 0:
                 nc.vector.tensor_scalar(res_flat, acc[:], b1_sb[:, 0:1], None, ADD)
-                nc.sync.dma_start(out_blocks[0], res[:])
             else:
                 nc.scalar.activation(res_flat, acc[:], IDENTITY, bias=b1_sb[:, 1:2])
-                nc.scalar.dma_start(out_blocks[1], res[:])
+            queues[kb].dma_start(out_blocks[kb], res[:])

@@ -19,47 +19,49 @@ FLOPS = 2 * NODES * FEAT * HIDDEN * SAMPLES
 
 def tile_canonicalgraphadapter_kernel(tc, x, pw, lab_bias, w1, b1, offs, out):
     nc = tc.nc
-    queues = [nc.sync, nc.scalar]
     with (
         tc.tile_pool(name="held", bufs=1) as held,
         tc.psum_pool(name="psum", bufs=1) as psum,
     ):
-        x_sb = [held.tile([FEAT, SAMPLES], F32, name=f"x_sb{a}") for a in range(NODES)]
-        pw_sb = [held.tile([FEAT, NODES * SAMPLES], F32, name=f"pw_sb{a}") for a in range(NODES)]
-        for a in range(NODES):
-            queues[a].dma_start(x_sb[a][:], x[a * FEAT : (a + 1) * FEAT, :])
-            queues[1 - a].dma_start(pw_sb[a][:], pw[a].rearrange("e j -> (e j)").partition_broadcast(FEAT))
+        x_sb = held.tile([FEAT, NODES, SAMPLES], F32, name="x_sb")
+        nc.sync.dma_start(x_sb[:], x.rearrange("(a f) j -> f a j", f=FEAT))
+        pw_sb = held.tile([FEAT, NODES * NODES * SAMPLES], F32, name="pw_sb")
+        nc.scalar.dma_start(pw_sb[:], pw.rearrange("a e j -> (a e j)").partition_broadcast(FEAT))
         offsets = held.tile([128, SAMPLES // 16], U16, name="offsets")
         nc.sync.dma_start(offsets[:], offs)
         lab_sb = [held.tile([FEAT, LABS], F32, name=f"lab_sb{e}") for e in range(NODES)]
-        for e in range(NODES):
-            queues[e].dma_start(lab_sb[e][:], lab_bias[e * FEAT : (e + 1) * FEAT, :])
+        nc.sync.dma_start(lab_sb[0][:], lab_bias[0:FEAT, :])
+        nc.scalar.dma_start(lab_sb[1][:], lab_bias[FEAT : 2 * FEAT, :])
         w1_sb = held.tile([FEAT, HIDDEN], BF16, name="w1_sb")
         nc.scalar.dma_start(w1_sb[:], w1)
+        b1_row = held.tile([1, HIDDEN], F32, name="b1_row")
+        nc.gpsimd.dma_start(b1_row[:], b1.rearrange("k o -> o k"))
+
+        one = held.tile([1, 1], F32, name="one")
+        nc.vector.memset(one[:], 1.0)
+        b1_ps = psum.tile([128, KBLOCKS], F32, name="b1_ps")
+        for kb in range(KBLOCKS):
+            nc.tensor.matmul(b1_ps[:, kb : kb + 1], b1_row[:, kb * 128 : (kb + 1) * 128], one[:], start=True, stop=True)
         b1_sb = held.tile([128, KBLOCKS], F32, name="b1_sb")
-        with nc.allow_non_contiguous_dma(reason="256 bias values, one to a partition"):
-            nc.gpsimd.dma_start(b1_sb[:], b1.rearrange("(kb p) o -> p (kb o)", p=128))
+        nc.scalar.activation(b1_sb[:], b1_ps[:], IDENTITY)
 
-        warm = held.tile([128, 2], F32, name="warm")
-        nc.vector.memset(warm[:, 0:1], 0.0)
-        nc.scalar.activation(warm[:, 1:2], warm[:, 0:1], IDENTITY)
+        prod = held.tile([FEAT, NODES * NODES * SAMPLES], F32, name="prod")
+        nc.vector.tensor_tensor(
+            prod[:].rearrange("f (a e j) -> f a e j", a=NODES, e=NODES),
+            x_sb[:].unsqueeze(2).to_broadcast([FEAT, NODES, NODES, SAMPLES]),
+            pw_sb[:].rearrange("f (a e j) -> f a e j", a=NODES, e=NODES),
+            MULT,
+        )
+        half = NODES * SAMPLES
+        mix = held.tile([FEAT, NODES * SAMPLES], F32, name="mix")
+        nc.vector.tensor_tensor(mix[:], prod[:, 0:half], prod[:, half : 2 * half], ADD)
 
-        prod = [held.tile([FEAT, NODES, SAMPLES], F32, name=f"prod{a}") for a in range(NODES)]
-        for a in range(NODES):
-            nc.vector.tensor_tensor(
-                prod[a][:],
-                x_sb[a][:].unsqueeze(1).to_broadcast([FEAT, NODES, SAMPLES]),
-                pw_sb[a][:].rearrange("f (e j) -> f e j", e=NODES),
-                MULT,
-            )
-        mix = held.tile([FEAT, NODES, SAMPLES], F32, name="mix")
-        nc.vector.tensor_tensor(mix[:], prod[0][:], prod[1][:], ADD)
-
-        y32 = held.tile([FEAT, NODES, SAMPLES], F32, name="y32")
+        y32 = held.tile([FEAT, NODES * SAMPLES], F32, name="y32")
         for e in range(NODES):
-            nc.vector.tensor_tensor(y32[:, e, :], lab_sb[e][:].indirect(offsets[:]), mix[:, e, :], ADD)
+            cols = slice(e * SAMPLES, (e + 1) * SAMPLES)
+            nc.vector.tensor_tensor(y32[:, cols], lab_sb[e][:].indirect(offsets[:]), mix[:, cols], ADD)
         y_bf = held.tile([FEAT, NODES * SAMPLES], BF16, name="y_bf")
-        nc.vector.tensor_copy(y_bf[:], y32[:].rearrange("f e j -> f (e j)"))
+        nc.vector.tensor_copy(y_bf[:], y32[:])
 
         out_blocks = out.rearrange("(e kb p) j -> kb p e j", e=NODES, kb=KBLOCKS)
         for kb in range(KBLOCKS):
@@ -69,6 +71,7 @@ def tile_canonicalgraphadapter_kernel(tc, x, pw, lab_bias, w1, b1, offs, out):
             res_flat = res[:].rearrange("p e j -> p (e j)")
             if kb == 0:
                 nc.vector.tensor_scalar(res_flat, acc[:], b1_sb[:, 0:1], None, ADD)
+                nc.sync.dma_start(out_blocks[0], res[:])
             else:
                 nc.scalar.activation(res_flat, acc[:], IDENTITY, bias=b1_sb[:, 1:2])
-            queues[kb].dma_start(out_blocks[kb], res[:])
+                nc.scalar.dma_start(out_blocks[1], res[:])

@@ -34,16 +34,9 @@ def tile_canonicalgraphadapter_kernel(tc, x, pw, lab_bias, w1, b1, offs, out):
         nc.scalar.dma_start(lab_sb[1][:], lab_bias[FEAT : 2 * FEAT, :])
         w1_sb = held.tile([FEAT, HIDDEN], BF16, name="w1_sb")
         nc.scalar.dma_start(w1_sb[:], w1)
-        b1_row = held.tile([1, HIDDEN], F32, name="b1_row")
-        nc.gpsimd.dma_start(b1_row[:], b1.rearrange("k o -> o k"))
-
-        one = held.tile([1, 1], F32, name="one")
-        nc.vector.memset(one[:], 1.0)
-        b1_ps = psum.tile([128, KBLOCKS], F32, name="b1_ps")
-        for kb in range(KBLOCKS):
-            nc.tensor.matmul(b1_ps[:, kb : kb + 1], b1_row[:, kb * 128 : (kb + 1) * 128], one[:], start=True, stop=True)
         b1_sb = held.tile([128, KBLOCKS], F32, name="b1_sb")
-        nc.scalar.activation(b1_sb[:], b1_ps[:], IDENTITY)
+        with nc.allow_non_contiguous_dma(reason="256 bias values, one to a partition"):
+            nc.gpsimd.dma_start(b1_sb[:], b1.rearrange("(kb p) o -> p (kb o)", p=128))
 
         prod = held.tile([FEAT, NODES * NODES * SAMPLES], F32, name="prod")
         nc.vector.tensor_tensor(
@@ -56,22 +49,25 @@ def tile_canonicalgraphadapter_kernel(tc, x, pw, lab_bias, w1, b1, offs, out):
         mix = held.tile([FEAT, NODES * SAMPLES], F32, name="mix")
         nc.vector.tensor_tensor(mix[:], prod[:, 0:half], prod[:, half : 2 * half], ADD)
 
-        y32 = held.tile([FEAT, NODES * SAMPLES], F32, name="y32")
+        y_bf = [held.tile([FEAT, SAMPLES], BF16, name=f"y_bf{e}") for e in range(NODES)]
         for e in range(NODES):
-            cols = slice(e * SAMPLES, (e + 1) * SAMPLES)
-            nc.vector.tensor_tensor(y32[:, cols], lab_sb[e][:].indirect(offsets[:]), mix[:, cols], ADD)
-        y_bf = held.tile([FEAT, NODES * SAMPLES], BF16, name="y_bf")
-        nc.vector.tensor_copy(y_bf[:], y32[:])
-
-        out_blocks = out.rearrange("(e kb p) j -> kb p e j", e=NODES, kb=KBLOCKS)
-        for kb in range(KBLOCKS):
-            acc = psum.tile([128, NODES * SAMPLES], F32, name=f"acc{kb}")
-            nc.tensor.matmul(acc[:], w1_sb[:, kb * 128 : (kb + 1) * 128], y_bf[:], start=True, stop=True)
-            res = held.tile([128, NODES, SAMPLES], F32, name=f"res{kb}")
-            res_flat = res[:].rearrange("p e j -> p (e j)")
-            if kb == 0:
-                nc.vector.tensor_scalar(res_flat, acc[:], b1_sb[:, 0:1], None, ADD)
-                nc.sync.dma_start(out_blocks[0], res[:])
+            y32 = held.tile([FEAT, SAMPLES], F32, name=f"y32_{e}")
+            mix_e = mix[:, e * SAMPLES : (e + 1) * SAMPLES]
+            nc.vector.tensor_tensor(y32[:], lab_sb[e][:].indirect(offsets[:]), mix_e, ADD)
+            if e == 0:
+                nc.scalar.activation(y_bf[e][:], y32[:], IDENTITY)
             else:
-                nc.scalar.activation(res_flat, acc[:], IDENTITY, bias=b1_sb[:, 1:2])
-                nc.scalar.dma_start(out_blocks[1], res[:])
+                nc.vector.tensor_copy(y_bf[e][:], y32[:])
+
+        out_blocks = out.rearrange("(e kb p) j -> e kb p j", e=NODES, kb=KBLOCKS)
+        for e in range(NODES):
+            for kb in range(KBLOCKS):
+                acc = psum.tile([128, SAMPLES], F32, name=f"acc{e}{kb}")
+                nc.tensor.matmul(acc[:], w1_sb[:, kb * 128 : (kb + 1) * 128], y_bf[e][:], start=True, stop=True)
+                res = held.tile([128, SAMPLES], F32, name=f"res{e}{kb}")
+                if kb == 0:
+                    nc.vector.tensor_scalar(res[:], acc[:], b1_sb[:, 0:1], None, ADD)
+                    nc.sync.dma_start(out_blocks[e, kb], res[:])
+                else:
+                    nc.scalar.activation(res[:], acc[:], IDENTITY, bias=b1_sb[:, 1:2])
+                    nc.scalar.dma_start(out_blocks[e, kb], res[:])

@@ -34,9 +34,16 @@ def tile_canonicalgraphadapter_kernel(tc, x, pw, lab_bias, w1, b1, offs, out):
         nc.scalar.dma_start(lab_sb[1][:], lab_bias[FEAT : 2 * FEAT, :])
         w1_sb = held.tile([FEAT, HIDDEN], BF16, name="w1_sb")
         nc.scalar.dma_start(w1_sb[:], w1)
+        b1_row = held.tile([1, HIDDEN], F32, name="b1_row")
+        nc.sync.dma_start(b1_row[:], b1.rearrange("k o -> o k"))
+
+        one = held.tile([1, 1], F32, name="one")
+        nc.vector.memset(one[:], 1.0)
+        b1_ps = psum.tile([128, KBLOCKS], F32, name="b1_ps")
+        for kb in range(KBLOCKS):
+            nc.tensor.matmul(b1_ps[:, kb : kb + 1], b1_row[:, kb * 128 : (kb + 1) * 128], one[:], start=True, stop=True)
         b1_sb = held.tile([128, KBLOCKS], F32, name="b1_sb")
-        with nc.allow_non_contiguous_dma(reason="256 bias values, one to a partition"):
-            nc.gpsimd.dma_start(b1_sb[:], b1.rearrange("(kb p) o -> p (kb o)", p=128))
+        nc.scalar.activation(b1_sb[:], b1_ps[:], IDENTITY)
 
         prod = held.tile([FEAT, NODES * NODES * SAMPLES], F32, name="prod")
         nc.vector.tensor_tensor(
@@ -49,25 +56,23 @@ def tile_canonicalgraphadapter_kernel(tc, x, pw, lab_bias, w1, b1, offs, out):
         mix = held.tile([FEAT, NODES * SAMPLES], F32, name="mix")
         nc.vector.tensor_tensor(mix[:], prod[:, 0:half], prod[:, half : 2 * half], ADD)
 
-        y_bf = [held.tile([FEAT, SAMPLES], BF16, name=f"y_bf{e}") for e in range(NODES)]
+        y32 = held.tile([FEAT, NODES * SAMPLES], F32, name="y32")
         for e in range(NODES):
-            y32 = held.tile([FEAT, SAMPLES], F32, name=f"y32_{e}")
-            mix_e = mix[:, e * SAMPLES : (e + 1) * SAMPLES]
-            nc.vector.tensor_tensor(y32[:], lab_sb[e][:].indirect(offsets[:]), mix_e, ADD)
-            if e == 0:
-                nc.scalar.activation(y_bf[e][:], y32[:], IDENTITY)
-            else:
-                nc.vector.tensor_copy(y_bf[e][:], y32[:])
+            cols = slice(e * SAMPLES, (e + 1) * SAMPLES)
+            nc.vector.tensor_tensor(y32[:, cols], lab_sb[e][:].indirect(offsets[:]), mix[:, cols], ADD)
+        y_bf = held.tile([FEAT, NODES * SAMPLES], BF16, name="y_bf")
+        nc.vector.tensor_copy(y_bf[:], y32[:])
 
-        out_blocks = out.rearrange("(e kb p) j -> e kb p j", e=NODES, kb=KBLOCKS)
-        for e in range(NODES):
-            for kb in range(KBLOCKS):
-                acc = psum.tile([128, SAMPLES], F32, name=f"acc{e}{kb}")
-                nc.tensor.matmul(acc[:], w1_sb[:, kb * 128 : (kb + 1) * 128], y_bf[e][:], start=True, stop=True)
-                res = held.tile([128, SAMPLES], F32, name=f"res{e}{kb}")
-                if kb == 0:
-                    nc.vector.tensor_scalar(res[:], acc[:], b1_sb[:, 0:1], None, ADD)
-                    nc.sync.dma_start(out_blocks[e, kb], res[:])
-                else:
-                    nc.scalar.activation(res[:], acc[:], IDENTITY, bias=b1_sb[:, 1:2])
-                    nc.scalar.dma_start(out_blocks[e, kb], res[:])
+        res = held.tile([128, NODES, KBLOCKS, SAMPLES], F32, name="res")
+        for kb in range(KBLOCKS):
+            acc = psum.tile([128, NODES, SAMPLES], F32, name=f"acc{kb}")
+            nc.tensor.matmul(
+                acc[:].rearrange("p e j -> p (e j)"), w1_sb[:, kb * 128 : (kb + 1) * 128], y_bf[:], start=True, stop=True
+            )
+            if kb == 0:
+                nc.vector.tensor_scalar(res[:, :, kb, :], acc[:], b1_sb[:, 0:1], None, ADD)
+            else:
+                nc.scalar.activation(res[:, :, kb, :], acc[:], IDENTITY, bias=b1_sb[:, 1:2])
+        nc.sync.dma_start(
+            out.rearrange("(b p) j -> p b j", p=128), res[:].rearrange("p e kb j -> p (e kb) j")
+        )

@@ -34,45 +34,33 @@ def tile_canonicalgraphadapter_kernel(tc, x, pw, lab_bias, w1, b1, offs, out):
         nc.scalar.dma_start(lab_sb[1][:], lab_bias[FEAT : 2 * FEAT, :])
         w1_sb = held.tile([FEAT, HIDDEN], BF16, name="w1_sb")
         nc.scalar.dma_start(w1_sb[:], w1)
-        b1_row = held.tile([1, HIDDEN], F32, name="b1_row")
-        nc.sync.dma_start(b1_row[:], b1.rearrange("k o -> o k"))
-
-        one = held.tile([1, 1], F32, name="one")
-        nc.vector.memset(one[:], 1.0)
-        b1_ps = psum.tile([128, KBLOCKS], F32, name="b1_ps")
-        for kb in range(KBLOCKS):
-            nc.tensor.matmul(b1_ps[:, kb : kb + 1], b1_row[:, kb * 128 : (kb + 1) * 128], one[:], start=True, stop=True)
         b1_sb = held.tile([128, KBLOCKS], F32, name="b1_sb")
-        nc.scalar.activation(b1_sb[:], b1_ps[:], IDENTITY)
+        with nc.allow_non_contiguous_dma(reason="256 bias values, one to a partition"):
+            nc.gpsimd.dma_start(b1_sb[:], b1.rearrange("(kb p) o -> p (kb o)", p=128))
 
-        prod = held.tile([FEAT, NODES * NODES * SAMPLES], F32, name="prod")
-        nc.vector.tensor_tensor(
-            prod[:].rearrange("f (a e j) -> f a e j", a=NODES, e=NODES),
-            x_sb[:].unsqueeze(2).to_broadcast([FEAT, NODES, NODES, SAMPLES]),
-            pw_sb[:].rearrange("f (a e j) -> f a e j", a=NODES, e=NODES),
-            MULT,
-        )
-        half = NODES * SAMPLES
-        mix = held.tile([FEAT, NODES * SAMPLES], F32, name="mix")
-        nc.vector.tensor_tensor(mix[:], prod[:, 0:half], prod[:, half : 2 * half], ADD)
-
-        y32 = held.tile([FEAT, NODES * SAMPLES], F32, name="y32")
+        pw_by_node = pw_sb[:].rearrange("f (a e j) -> f a e j", a=NODES, e=NODES)
+        prod = [held.tile([FEAT, NODES, SAMPLES], F32, name=f"prod{e}") for e in range(NODES)]
         for e in range(NODES):
-            cols = slice(e * SAMPLES, (e + 1) * SAMPLES)
-            nc.vector.tensor_tensor(y32[:, cols], lab_sb[e][:].indirect(offsets[:]), mix[:, cols], ADD)
+            nc.vector.tensor_tensor(prod[e][:], x_sb[:], pw_by_node[:, :, e, :], MULT)
+        mix = [held.tile([FEAT, SAMPLES], F32, name=f"mix{e}") for e in range(NODES)]
+        for e in range(NODES):
+            nc.vector.tensor_tensor(mix[e][:], prod[e][:, 0, :], prod[e][:, 1, :], ADD)
+        y32 = [held.tile([FEAT, SAMPLES], F32, name=f"y32_{e}") for e in range(NODES)]
+        for e in range(NODES):
+            nc.vector.tensor_tensor(y32[e][:], lab_sb[e][:].indirect(offsets[:]), mix[e][:], ADD)
         y_bf = held.tile([FEAT, NODES * SAMPLES], BF16, name="y_bf")
-        nc.vector.tensor_copy(y_bf[:], y32[:])
+        for e in range(NODES):
+            nc.vector.tensor_copy(y_bf[:, e * SAMPLES : (e + 1) * SAMPLES], y32[e][:])
 
-        res = held.tile([128, NODES, KBLOCKS, SAMPLES], F32, name="res")
+        out_blocks = out.rearrange("(e kb p) j -> kb p e j", e=NODES, kb=KBLOCKS)
         for kb in range(KBLOCKS):
-            acc = psum.tile([128, NODES, SAMPLES], F32, name=f"acc{kb}")
-            nc.tensor.matmul(
-                acc[:].rearrange("p e j -> p (e j)"), w1_sb[:, kb * 128 : (kb + 1) * 128], y_bf[:], start=True, stop=True
-            )
+            acc = psum.tile([128, NODES * SAMPLES], F32, name=f"acc{kb}")
+            nc.tensor.matmul(acc[:], w1_sb[:, kb * 128 : (kb + 1) * 128], y_bf[:], start=True, stop=True)
+            res = held.tile([128, NODES, SAMPLES], F32, name=f"res{kb}")
+            res_flat = res[:].rearrange("p e j -> p (e j)")
             if kb == 0:
-                nc.vector.tensor_scalar(res[:, :, kb, :], acc[:], b1_sb[:, 0:1], None, ADD)
+                nc.vector.tensor_scalar(res_flat, acc[:], b1_sb[:, 0:1], None, ADD)
+                nc.sync.dma_start(out_blocks[0], res[:])
             else:
-                nc.scalar.activation(res[:, :, kb, :], acc[:], IDENTITY, bias=b1_sb[:, 1:2])
-        nc.sync.dma_start(
-            out.rearrange("(b p) j -> p b j", p=128), res[:].rearrange("p e kb j -> p (e kb) j")
-        )
+                nc.scalar.activation(res_flat, acc[:], IDENTITY, bias=b1_sb[:, 1:2])
+                nc.scalar.dma_start(out_blocks[1], res[:])

@@ -12,7 +12,7 @@ FEAT = 128
 HIDDEN = 256
 LABS = 256
 SAMPLES = 128
-KBLOCKS = HIDDEN // 128
+ROWS_PER_PART = HIDDEN // 128
 
 FLOPS = 2 * NODES * FEAT * HIDDEN * SAMPLES
 
@@ -34,9 +34,8 @@ def tile_canonicalgraphadapter_kernel(tc, x, pw, lab_bias, w1, b1, offs, out):
         nc.scalar.dma_start(lab_sb[1][:], lab_bias[FEAT : 2 * FEAT, :])
         w1_sb = held.tile([FEAT, HIDDEN], BF16, name="w1_sb")
         nc.scalar.dma_start(w1_sb[:], w1)
-        b1_sb = held.tile([128, KBLOCKS], F32, name="b1_sb")
-        with nc.allow_non_contiguous_dma(reason="256 bias values, one to a partition"):
-            nc.gpsimd.dma_start(b1_sb[:], b1.rearrange("(kb p) o -> p (kb o)", p=128))
+        b1_sb = held.tile([128, ROWS_PER_PART], F32, name="b1_sb")
+        nc.gpsimd.dma_start(b1_sb[:], b1.rearrange("(p r) o -> p (r o)", p=128))
 
         pw_by_node = pw_sb[:].rearrange("f (a e j) -> f a e j", a=NODES, e=NODES)
         prod = [held.tile([FEAT, NODES, SAMPLES], F32, name=f"prod{e}") for e in range(NODES)]
@@ -52,15 +51,15 @@ def tile_canonicalgraphadapter_kernel(tc, x, pw, lab_bias, w1, b1, offs, out):
         for e in range(NODES):
             nc.vector.tensor_copy(y_bf[:, e * SAMPLES : (e + 1) * SAMPLES], y32[e][:])
 
-        out_blocks = out.rearrange("(e kb p) j -> kb p e j", e=NODES, kb=KBLOCKS)
-        for kb in range(KBLOCKS):
-            acc = psum.tile([128, NODES * SAMPLES], F32, name=f"acc{kb}")
-            nc.tensor.matmul(acc[:], w1_sb[:, kb * 128 : (kb + 1) * 128], y_bf[:], start=True, stop=True)
-            res = held.tile([128, NODES, SAMPLES], F32, name=f"res{kb}")
-            res_flat = res[:].rearrange("p e j -> p (e j)")
-            if kb == 0:
-                nc.vector.tensor_scalar(res_flat, acc[:], b1_sb[:, 0:1], None, ADD)
-                nc.sync.dma_start(out_blocks[0], res[:])
+        w1_by_r = w1_sb[:].rearrange("f (p r) -> f r p", r=ROWS_PER_PART)
+        res = held.tile([128, NODES, ROWS_PER_PART, SAMPLES], F32, name="res")
+        for r in range(ROWS_PER_PART):
+            acc = psum.tile([128, NODES, SAMPLES], F32, name=f"acc{r}")
+            nc.tensor.matmul(acc[:].rearrange("p e j -> p (e j)"), w1_by_r[:, r, :], y_bf[:], start=True, stop=True)
+            if r == 0:
+                nc.vector.tensor_scalar(res[:, :, 0, :], acc[:], b1_sb[:, 0:1], None, ADD)
             else:
-                nc.scalar.activation(res_flat, acc[:], IDENTITY, bias=b1_sb[:, 1:2])
-                nc.scalar.dma_start(out_blocks[1], res[:])
+                nc.scalar.activation(res[:, :, 1, :], acc[:], IDENTITY, bias=b1_sb[:, 1:2])
+        out_by_node = out.rearrange("(e p r) j -> e p (r j)", e=NODES, r=ROWS_PER_PART)
+        nc.sync.dma_start(out_by_node[0], res[:, 0, :, :].rearrange("p r j -> p (r j)"))
+        nc.scalar.dma_start(out_by_node[1], res[:, 1, :, :].rearrange("p r j -> p (r j)"))

@@ -39,27 +39,38 @@ def tile_canonicalgraphadapter_kernel(tc, x, pw, lab_bias, w1, b1, offs, out):
 
         pw_by_node = pw_sb[:].rearrange("f (a e j) -> f a e j", a=NODES, e=NODES)
         prod = [held.tile([FEAT, NODES, SAMPLES], F32, name=f"prod{e}") for e in range(NODES)]
-        for e in range(NODES):
-            nc.vector.tensor_tensor(prod[e][:], x_sb[:], pw_by_node[:, :, e, :], MULT)
         mix = [held.tile([FEAT, SAMPLES], F32, name=f"mix{e}") for e in range(NODES)]
-        for e in range(NODES):
-            nc.vector.tensor_tensor(mix[e][:], prod[e][:, 0, :], prod[e][:, 1, :], ADD)
         y32 = [held.tile([FEAT, SAMPLES], F32, name=f"y32_{e}") for e in range(NODES)]
-        for e in range(NODES):
+        y_bf = [held.tile([FEAT, SAMPLES], BF16, name=f"y_bf{e}") for e in range(NODES)]
+
+        def product(e):
+            nc.vector.tensor_tensor(prod[e][:], x_sb[:], pw_by_node[:, :, e, :], MULT)
+
+        def total(e):
+            nc.vector.tensor_tensor(mix[e][:], prod[e][:, 0, :], prod[e][:, 1, :], ADD)
+
+        def look_up_and_add(e):
             nc.vector.tensor_tensor(y32[e][:], lab_sb[e][:].indirect(offsets[:]), mix[e][:], ADD)
-        y_bf = held.tile([FEAT, NODES * SAMPLES], BF16, name="y_bf")
-        for e in range(NODES):
-            nc.vector.tensor_copy(y_bf[:, e * SAMPLES : (e + 1) * SAMPLES], y32[e][:])
+
+        def round_to_bf16(e):
+            nc.vector.tensor_copy(y_bf[e][:], y32[e][:])
+
+        product(0)
+        product(1)
+        total(0)
+        look_up_and_add(0)
+        total(1)
+        round_to_bf16(0)
+        look_up_and_add(1)
+        round_to_bf16(1)
 
         w1_by_r = w1_sb[:].rearrange("f (p r) -> f r p", r=ROWS_PER_PART)
-        res = held.tile([128, NODES, ROWS_PER_PART, SAMPLES], F32, name="res")
-        for r in range(ROWS_PER_PART):
-            acc = psum.tile([128, NODES, SAMPLES], F32, name=f"acc{r}")
-            nc.tensor.matmul(acc[:].rearrange("p e j -> p (e j)"), w1_by_r[:, r, :], y_bf[:], start=True, stop=True)
-            if r == 0:
-                nc.vector.tensor_scalar(res[:, :, 0, :], acc[:], b1_sb[:, 0:1], None, ADD)
-            else:
-                nc.scalar.activation(res[:, :, 1, :], acc[:], IDENTITY, bias=b1_sb[:, 1:2])
         out_by_node = out.rearrange("(e p r) j -> e p (r j)", e=NODES, r=ROWS_PER_PART)
-        nc.sync.dma_start(out_by_node[0], res[:, 0, :, :].rearrange("p r j -> p (r j)"))
-        nc.scalar.dma_start(out_by_node[1], res[:, 1, :, :].rearrange("p r j -> p (r j)"))
+        for e in range(NODES):
+            res = held.tile([128, ROWS_PER_PART, SAMPLES], F32, name=f"res{e}")
+            acc = [psum.tile([128, SAMPLES], F32, name=f"acc{e}_{r}") for r in range(ROWS_PER_PART)]
+            for r in range(ROWS_PER_PART):
+                nc.tensor.matmul(acc[r][:], w1_by_r[:, r, :], y_bf[e][:], start=True, stop=True)
+            nc.vector.tensor_scalar(res[:, 0, :], acc[0][:], b1_sb[:, 0:1], None, ADD)
+            nc.scalar.activation(res[:, 1, :], acc[1][:], IDENTITY, bias=b1_sb[:, 1:2])
+            nc.sync.dma_start(out_by_node[e], res[:].rearrange("p r j -> p (r j)"))

@@ -30,8 +30,8 @@ def tile_canonicalgraphadapter_kernel(tc, x, pw, lab_bias, w1, b1, offs, out):
         offsets = held.tile([128, SAMPLES // 16], U16, name="offsets")
         nc.sync.dma_start(offsets[:], offs)
         lab_sb = [held.tile([FEAT, LABS], F32, name=f"lab_sb{e}") for e in range(NODES)]
-        nc.sync.dma_start(lab_sb[0][:], lab_bias[0:FEAT, :])
-        nc.scalar.dma_start(lab_sb[1][:], lab_bias[FEAT : 2 * FEAT, :])
+        nc.scalar.dma_start(lab_sb[0][:], lab_bias[0:FEAT, :])
+        nc.sync.dma_start(lab_sb[1][:], lab_bias[FEAT : 2 * FEAT, :])
         w1_sb = held.tile([FEAT, HIDDEN], BF16, name="w1_sb")
         nc.scalar.dma_start(w1_sb[:], w1)
         b1_sb = held.tile([128, ROWS_PER_PART], F32, name="b1_sb")

@@ -69,7 +69,7 @@ def tile_canonicalgraphadapter_kernel(tc, x, pw, lab_bias, w1, b1, offs, out):
         for e in range(NODES):
             res = held.tile([128, ROWS_PER_PART, SAMPLES], F32, name=f"res{e}")
             acc = [psum.tile([128, SAMPLES], F32, name=f"acc{e}_{r}") for r in range(ROWS_PER_PART)]
-            for r in range(ROWS_PER_PART):
+            for r in reversed(range(ROWS_PER_PART)):
                 nc.tensor.matmul(acc[r][:], w1_by_r[:, r, :], y_bf[e][:], start=True, stop=True)
             nc.vector.tensor_scalar(res[:, 0, :], acc[0][:], b1_sb[:, 0:1], None, ADD)
             nc.scalar.activation(res[:, 1, :], acc[1][:], IDENTITY, bias=b1_sb[:, 1:2])

@@ -37,6 +37,11 @@ def tile_canonicalgraphadapter_kernel(tc, x, pw, lab_bias, w1, b1, offs, out):
         b1_sb = held.tile([128, ROWS_PER_PART], F32, name="b1_sb")
         nc.gpsimd.dma_start(b1_sb[:], b1.rearrange("(p r) o -> p (r o)", p=128))
 
+        zero = held.tile([128, 1], F32, name="zero")
+        nc.vector.memset(zero[:], 0.0)
+        warmed = held.tile([128, 1], F32, name="warmed")
+        nc.scalar.activation(warmed[:], zero[:], IDENTITY)
+
         pw_by_node = pw_sb[:].rearrange("f (a e j) -> f a e j", a=NODES, e=NODES)
         prod = [held.tile([FEAT, NODES, SAMPLES], F32, name=f"prod{e}") for e in range(NODES)]
         mix = [held.tile([FEAT, SAMPLES], F32, name=f"mix{e}") for e in range(NODES)]

@@ -25,8 +25,8 @@ def tile_canonicalgraphadapter_kernel(tc, x, pw, lab_bias, w1, b1, offs, out):
     ):
         x_sb = held.tile([FEAT, NODES, SAMPLES], F32, name="x_sb")
         nc.sync.dma_start(x_sb[:], x.rearrange("(a f) j -> f a j", f=FEAT))
-        pw_sb = held.tile([FEAT, NODES * NODES * SAMPLES], F32, name="pw_sb")
-        nc.scalar.dma_start(pw_sb[:], pw.rearrange("a e j -> (a e j)").partition_broadcast(FEAT))
+        pw_row = held.tile([1, NODES, NODES, SAMPLES], F32, name="pw_row")
+        nc.scalar.dma_start(pw_row[:], pw.rearrange("(o a) e j -> o e a j", o=1))
         offsets = held.tile([128, SAMPLES // 16], U16, name="offsets")
         nc.sync.dma_start(offsets[:], offs)
         lab_sb = [held.tile([FEAT, LABS], F32, name=f"lab_sb{e}") for e in range(NODES)]
@@ -42,14 +42,24 @@ def tile_canonicalgraphadapter_kernel(tc, x, pw, lab_bias, w1, b1, offs, out):
         warmed = held.tile([128, 1], F32, name="warmed")
         nc.scalar.activation(warmed[:], zero[:], IDENTITY)
 
-        pw_by_node = pw_sb[:].rearrange("f (a e j) -> f a e j", a=NODES, e=NODES)
+        ones = held.tile([1, FEAT], F32, name="ones")
+        nc.vector.memset(ones[:], 1.0)
+        pw_all = [psum.tile([FEAT, NODES, SAMPLES], F32, name=f"pw_all{e}") for e in range(NODES)]
+        for e in range(NODES):
+            nc.tensor.matmul(
+                pw_all[e][:].rearrange("f a j -> f (a j)"),
+                ones[:],
+                pw_row[:, e, :, :].rearrange("o a j -> o (a j)"),
+                start=True,
+                stop=True,
+            )
         prod = [held.tile([FEAT, NODES, SAMPLES], F32, name=f"prod{e}") for e in range(NODES)]
         mix = [held.tile([FEAT, SAMPLES], F32, name=f"mix{e}") for e in range(NODES)]
         y32 = [held.tile([FEAT, SAMPLES], F32, name=f"y32_{e}") for e in range(NODES)]
         y_bf = [held.tile([FEAT, SAMPLES], BF16, name=f"y_bf{e}") for e in range(NODES)]
 
         def product(e):
-            nc.vector.tensor_tensor(prod[e][:], x_sb[:], pw_by_node[:, :, e, :], MULT)
+            nc.vector.tensor_tensor(prod[e][:], x_sb[:], pw_all[e][:], MULT)
 
         def total(e):
             nc.vector.tensor_tensor(mix[e][:], prod[e][:, 0, :], prod[e][:, 1, :], ADD)
@@ -60,14 +70,11 @@ def tile_canonicalgraphadapter_kernel(tc, x, pw, lab_bias, w1, b1, offs, out):
         def round_to_bf16(e):
             nc.vector.tensor_copy(y_bf[e][:], y32[e][:])
 
-        product(0)
-        product(1)
-        total(0)
-        look_up_and_add(0)
-        total(1)
-        round_to_bf16(0)
-        look_up_and_add(1)
-        round_to_bf16(1)
+        for e in range(NODES):
+            product(e)
+            total(e)
+            look_up_and_add(e)
+            round_to_bf16(e)
 
         w1_by_r = w1_sb[:].rearrange("f (p r) -> f r p", r=ROWS_PER_PART)
         out_by_node = out.rearrange("(e p r) j -> e p (r j)", e=NODES, r=ROWS_PER_PART)

@@ -23,10 +23,10 @@ def tile_canonicalgraphadapter_kernel(tc, x, pw, lab_bias, w1, b1, offs, out):
         tc.tile_pool(name="held", bufs=1) as held,
         tc.psum_pool(name="psum", bufs=1) as psum,
     ):
-        x_sb = held.tile([FEAT, NODES, SAMPLES], F32, name="x_sb")
-        nc.sync.dma_start(x_sb[:], x.rearrange("(a f) j -> f a j", f=FEAT))
         pw_row = held.tile([1, NODES, NODES, SAMPLES], F32, name="pw_row")
-        nc.scalar.dma_start(pw_row[:], pw.rearrange("(o a) e j -> o e a j", o=1))
+        nc.sync.dma_start(pw_row[:], pw.rearrange("(o a) e j -> o e a j", o=1))
+        x_sb = held.tile([FEAT, NODES, SAMPLES], F32, name="x_sb")
+        nc.scalar.dma_start(x_sb[:], x.rearrange("(a f) j -> f a j", f=FEAT))
         offsets = held.tile([128, SAMPLES // 16], U16, name="offsets")
         nc.sync.dma_start(offsets[:], offs)
         lab_sb = [held.tile([FEAT, LABS], F32, name=f"lab_sb{e}") for e in range(NODES)]
@@ -44,22 +44,20 @@ def tile_canonicalgraphadapter_kernel(tc, x, pw, lab_bias, w1, b1, offs, out):
 
         ones = held.tile([1, FEAT], F32, name="ones")
         nc.vector.memset(ones[:], 1.0)
-        pw_all = [psum.tile([FEAT, NODES, SAMPLES], F32, name=f"pw_all{e}") for e in range(NODES)]
+        pw_all = [
+            [psum.tile([FEAT, SAMPLES], F32, name=f"pw_all{e}_{a}") for a in range(NODES)] for e in range(NODES)
+        ]
         for e in range(NODES):
-            nc.tensor.matmul(
-                pw_all[e][:].rearrange("f a j -> f (a j)"),
-                ones[:],
-                pw_row[:, e, :, :].rearrange("o a j -> o (a j)"),
-                start=True,
-                stop=True,
-            )
+            for a in range(NODES):
+                nc.tensor.matmul(pw_all[e][a][:], ones[:], pw_row[:, e, a, :], start=True, stop=True)
         prod = [held.tile([FEAT, NODES, SAMPLES], F32, name=f"prod{e}") for e in range(NODES)]
         mix = [held.tile([FEAT, SAMPLES], F32, name=f"mix{e}") for e in range(NODES)]
         y32 = [held.tile([FEAT, SAMPLES], F32, name=f"y32_{e}") for e in range(NODES)]
         y_bf = [held.tile([FEAT, SAMPLES], BF16, name=f"y_bf{e}") for e in range(NODES)]
 
         def product(e):
-            nc.vector.tensor_tensor(prod[e][:], x_sb[:], pw_all[e][:], MULT)
+            for a in range(NODES):
+                nc.vector.tensor_tensor(prod[e][:, a, :], x_sb[:, a, :], pw_all[e][a][:], MULT)
 
         def total(e):
             nc.vector.tensor_tensor(mix[e][:], prod[e][:, 0, :], prod[e][:, 1, :], ADD)

@@ -5,6 +5,7 @@ BF16 = mybir.dt.bfloat16
 U16 = mybir.dt.uint16
 MULT = mybir.AluOpType.mult
 ADD = mybir.AluOpType.add
+SUBTRACT = mybir.AluOpType.subtract
 IDENTITY = mybir.ActivationFunctionType.Identity
 
 NODES = 2
@@ -42,22 +43,36 @@ def tile_canonicalgraphadapter_kernel(tc, x, pw, lab_bias, w1, b1, offs, out):
         warmed = held.tile([128, 1], F32, name="warmed")
         nc.scalar.activation(warmed[:], zero[:], IDENTITY)
 
-        ones = held.tile([1, FEAT], F32, name="ones")
+        ones = held.tile([1, FEAT], BF16, name="ones")
         nc.vector.memset(ones[:], 1.0)
-        pw_all = [
-            [psum.tile([FEAT, SAMPLES], F32, name=f"pw_all{e}_{a}") for a in range(NODES)] for e in range(NODES)
-        ]
-        for e in range(NODES):
-            for a in range(NODES):
-                nc.tensor.matmul(pw_all[e][a][:], ones[:], pw_row[:, e, a, :], start=True, stop=True)
+        rest1 = held.tile([1, NODES, NODES, SAMPLES], F32, name="rest1")
+        rest2 = held.tile([1, NODES, NODES, SAMPLES], F32, name="rest2")
+
+        def upper(tile, e):
+            halves = tile[:].bitcast(BF16).rearrange("o e a (j two) -> o e (a j) two", two=2)
+            return halves[:, e, :, 1]
+
+        def words(tile, e):
+            return tile[:].rearrange("o e a j -> o e (a j)")[:, e, :]
+
+        for whole, rest in ((pw_row, rest1), (rest1, rest2)):
+            for e in range(NODES):
+                nc.vector.tensor_tensor(words(rest, e), words(whole, e), upper(whole, e), SUBTRACT)
+        pw_all = [psum.tile([FEAT, NODES, SAMPLES], F32, name=f"pw_all{e}") for e in range(NODES)]
+        for part in (pw_row, rest1, rest2):
+            for e in range(NODES):
+                nc.tensor.matmul(
+                    pw_all[e][:].rearrange("f a j -> f (a j)"), ones[:], upper(part, e),
+                    start=part is pw_row, stop=part is rest2,
+                )
+
         prod = [held.tile([FEAT, NODES, SAMPLES], F32, name=f"prod{e}") for e in range(NODES)]
         mix = [held.tile([FEAT, SAMPLES], F32, name=f"mix{e}") for e in range(NODES)]
         y32 = [held.tile([FEAT, SAMPLES], F32, name=f"y32_{e}") for e in range(NODES)]
         y_bf = [held.tile([FEAT, SAMPLES], BF16, name=f"y_bf{e}") for e in range(NODES)]
 
         def product(e):
-            for a in range(NODES):
-                nc.vector.tensor_tensor(prod[e][:, a, :], x_sb[:, a, :], pw_all[e][a][:], MULT)
+            nc.vector.tensor_tensor(prod[e][:], x_sb[:], pw_all[e][:], MULT)
 
         def total(e):
             nc.vector.tensor_tensor(mix[e][:], prod[e][:, 0, :], prod[e][:, 1, :], ADD)

@@ -24,10 +24,11 @@ def tile_canonicalgraphadapter_kernel(tc, x, pw, lab_bias, w1, b1, offs, out):
         tc.tile_pool(name="held", bufs=1) as held,
         tc.psum_pool(name="psum", bufs=1) as psum,
     ):
-        pw_row = held.tile([1, NODES, NODES, SAMPLES], F32, name="pw_row")
-        nc.sync.dma_start(pw_row[:], pw.rearrange("(o a) e j -> o e a j", o=1))
+        pw_rows = [held.tile([NODES, SAMPLES], F32, name=f"pw_rows{e}") for e in range(NODES)]
+        nc.sync.dma_start(pw_rows[0][:], pw[:, 0, :])
+        nc.scalar.dma_start(pw_rows[1][:], pw[:, 1, :])
         x_sb = held.tile([FEAT, NODES, SAMPLES], F32, name="x_sb")
-        nc.scalar.dma_start(x_sb[:], x.rearrange("(a f) j -> f a j", f=FEAT))
+        nc.sync.dma_start(x_sb[:], x.rearrange("(a f) j -> f a j", f=FEAT))
         offsets = held.tile([128, SAMPLES // 16], U16, name="offsets")
         nc.sync.dma_start(offsets[:], offs)
         lab_sb = [held.tile([FEAT, LABS], F32, name=f"lab_sb{e}") for e in range(NODES)]
@@ -43,28 +44,26 @@ def tile_canonicalgraphadapter_kernel(tc, x, pw, lab_bias, w1, b1, offs, out):
         warmed = held.tile([128, 1], F32, name="warmed")
         nc.scalar.activation(warmed[:], zero[:], IDENTITY)
 
-        ones = held.tile([1, FEAT], BF16, name="ones")
-        nc.vector.memset(ones[:], 1.0)
-        rest1 = held.tile([1, NODES, NODES, SAMPLES], F32, name="rest1")
-        rest2 = held.tile([1, NODES, NODES, SAMPLES], F32, name="rest2")
+        pick = [held.tile([NODES, FEAT], BF16, name=f"pick{a}") for a in range(NODES)]
+        for a in range(NODES):
+            nc.vector.memset(pick[a][:], float(a == 1))
+            nc.vector.memset(pick[a][0:1, :], float(a == 0))
 
-        def upper(tile, e):
-            halves = tile[:].bitcast(BF16).rearrange("o e a (j two) -> o e (a j) two", two=2)
-            return halves[:, e, :, 1]
+        def upper(tile):
+            return tile[:].bitcast(BF16).rearrange("a (j two) -> a j two", two=2)[:, :, 1]
 
-        def words(tile, e):
-            return tile[:].rearrange("o e a j -> o e (a j)")[:, e, :]
-
-        for whole, rest in ((pw_row, rest1), (rest1, rest2)):
-            for e in range(NODES):
-                nc.vector.tensor_tensor(words(rest, e), words(whole, e), upper(whole, e), SUBTRACT)
-        pw_all = [psum.tile([FEAT, NODES, SAMPLES], F32, name=f"pw_all{e}") for e in range(NODES)]
-        for part in (pw_row, rest1, rest2):
-            for e in range(NODES):
-                nc.tensor.matmul(
-                    pw_all[e][:].rearrange("f a j -> f (a j)"), ones[:], upper(part, e),
-                    start=part is pw_row, stop=part is rest2,
-                )
+        pw_all = [
+            [psum.tile([FEAT, SAMPLES], F32, name=f"pw_all{e}_{a}") for a in range(NODES)] for e in range(NODES)
+        ]
+        for e in range(NODES):
+            parts = [pw_rows[e]]
+            for k in range(2):
+                rest = held.tile([NODES, SAMPLES], F32, name=f"rest{e}_{k}")
+                nc.vector.tensor_tensor(rest[:], parts[k][:], upper(parts[k]), SUBTRACT)
+                parts.append(rest)
+            for k in range(3):
+                for a in range(NODES):
+                    nc.tensor.matmul(pw_all[e][a][:], pick[a][:], upper(parts[k]), start=k == 0, stop=k == 2)
 
         prod = [held.tile([FEAT, NODES, SAMPLES], F32, name=f"prod{e}") for e in range(NODES)]
         mix = [held.tile([FEAT, SAMPLES], F32, name=f"mix{e}") for e in range(NODES)]
@@ -72,7 +71,8 @@ def tile_canonicalgraphadapter_kernel(tc, x, pw, lab_bias, w1, b1, offs, out):
         y_bf = [held.tile([FEAT, SAMPLES], BF16, name=f"y_bf{e}") for e in range(NODES)]
 
         def product(e):
-            nc.vector.tensor_tensor(prod[e][:], x_sb[:], pw_all[e][:], MULT)
+            for a in range(NODES):
+                nc.vector.tensor_tensor(prod[e][:, a, :], x_sb[:, a, :], pw_all[e][a][:], MULT)
 
         def total(e):
             nc.vector.tensor_tensor(mix[e][:], prod[e][:, 0, :], prod[e][:, 1, :], ADD)

@@ -13,6 +13,7 @@ FEAT = 128
 HIDDEN = 256
 LABS = 256
 SAMPLES = 128
+PAIRS = NODES * NODES
 ROWS_PER_PART = HIDDEN // 128
 
 FLOPS = 2 * NODES * FEAT * HIDDEN * SAMPLES
@@ -24,11 +25,10 @@ def tile_canonicalgraphadapter_kernel(tc, x, pw, lab_bias, w1, b1, offs, out):
         tc.tile_pool(name="held", bufs=1) as held,
         tc.psum_pool(name="psum", bufs=1) as psum,
     ):
-        pw_rows = [held.tile([NODES, SAMPLES], F32, name=f"pw_rows{e}") for e in range(NODES)]
-        nc.sync.dma_start(pw_rows[0][:], pw[:, 0, :])
-        nc.scalar.dma_start(pw_rows[1][:], pw[:, 1, :])
+        pw_rows = held.tile([PAIRS, SAMPLES], F32, name="pw_rows")
+        nc.sync.dma_start(pw_rows[:], pw.rearrange("a e j -> (a e) j"))
         x_sb = held.tile([FEAT, NODES, SAMPLES], F32, name="x_sb")
-        nc.sync.dma_start(x_sb[:], x.rearrange("(a f) j -> f a j", f=FEAT))
+        nc.scalar.dma_start(x_sb[:], x.rearrange("(a f) j -> f a j", f=FEAT))
         offsets = held.tile([128, SAMPLES // 16], U16, name="offsets")
         nc.sync.dma_start(offsets[:], offs)
         lab_sb = [held.tile([FEAT, LABS], F32, name=f"lab_sb{e}") for e in range(NODES)]
@@ -44,26 +44,28 @@ def tile_canonicalgraphadapter_kernel(tc, x, pw, lab_bias, w1, b1, offs, out):
         warmed = held.tile([128, 1], F32, name="warmed")
         nc.scalar.activation(warmed[:], zero[:], IDENTITY)
 
-        pick = [held.tile([NODES, FEAT], BF16, name=f"pick{a}") for a in range(NODES)]
-        for a in range(NODES):
-            nc.vector.memset(pick[a][:], float(a == 1))
-            nc.vector.memset(pick[a][0:1, :], float(a == 0))
+        pick = [held.tile([PAIRS, FEAT], BF16, name=f"pick{i}") for i in range(PAIRS)]
+        for i in range(PAIRS):
+            nc.vector.memset(pick[i][:], 0.0)
+            nc.vector.memset(pick[i][0 : i + 1, :], 1.0)
+            if i > 0:
+                nc.vector.memset(pick[i][0:i, :], 0.0)
 
         def upper(tile):
-            return tile[:].bitcast(BF16).rearrange("a (j two) -> a j two", two=2)[:, :, 1]
+            return tile[:].bitcast(BF16).rearrange("i (j two) -> i j two", two=2)[:, :, 1]
 
+        parts = [pw_rows] + [held.tile([PAIRS, SAMPLES], F32, name=f"rest{k}") for k in range(2)]
+        for k in range(2):
+            nc.vector.tensor_tensor(parts[k + 1][:], parts[k][:], upper(parts[k]), SUBTRACT)
         pw_all = [
             [psum.tile([FEAT, SAMPLES], F32, name=f"pw_all{e}_{a}") for a in range(NODES)] for e in range(NODES)
         ]
         for e in range(NODES):
-            parts = [pw_rows[e]]
-            for k in range(2):
-                rest = held.tile([NODES, SAMPLES], F32, name=f"rest{e}_{k}")
-                nc.vector.tensor_tensor(rest[:], parts[k][:], upper(parts[k]), SUBTRACT)
-                parts.append(rest)
             for k in range(3):
                 for a in range(NODES):
-                    nc.tensor.matmul(pw_all[e][a][:], pick[a][:], upper(parts[k]), start=k == 0, stop=k == 2)
+                    nc.tensor.matmul(
+                        pw_all[e][a][:], pick[2 * a + e][:], upper(parts[k]), start=k == 0, stop=k == 2
+                    )
 
         prod = [held.tile([FEAT, NODES, SAMPLES], F32, name=f"prod{e}") for e in range(NODES)]
         mix = [held.tile([FEAT, SAMPLES], F32, name=f"mix{e}") for e in range(NODES)]

@@ -14,6 +14,7 @@ HIDDEN = 256
 LABS = 256
 SAMPLES = 128
 PAIRS = NODES * NODES
+COPIES = 2
 ROWS_PER_PART = HIDDEN // 128
 
 FLOPS = 2 * NODES * FEAT * HIDDEN * SAMPLES
@@ -25,8 +26,9 @@ def tile_canonicalgraphadapter_kernel(tc, x, pw, lab_bias, w1, b1, offs, out):
         tc.tile_pool(name="held", bufs=1) as held,
         tc.psum_pool(name="psum", bufs=1) as psum,
     ):
-        pw_rows = held.tile([PAIRS, SAMPLES], F32, name="pw_rows")
-        nc.sync.dma_start(pw_rows[:], pw.rearrange("a e j -> (a e) j"))
+        pw_rows = held.tile([COPIES * PAIRS, SAMPLES], F32, name="pw_rows")
+        nc.sync.dma_start(pw_rows[0:PAIRS, :], pw.rearrange("a e j -> (a e) j"))
+        nc.scalar.dma_start(pw_rows[PAIRS : COPIES * PAIRS, :], pw.rearrange("a e j -> (a e) j"))
         x_sb = held.tile([FEAT, NODES, SAMPLES], F32, name="x_sb")
         nc.scalar.dma_start(x_sb[:], x.rearrange("(a f) j -> f a j", f=FEAT))
         offsets = held.tile([128, SAMPLES // 16], U16, name="offsets")
@@ -35,7 +37,7 @@ def tile_canonicalgraphadapter_kernel(tc, x, pw, lab_bias, w1, b1, offs, out):
         nc.scalar.dma_start(lab_sb[0][:], lab_bias[0:FEAT, :])
         nc.sync.dma_start(lab_sb[1][:], lab_bias[FEAT : 2 * FEAT, :])
         w1_sb = held.tile([FEAT, HIDDEN], BF16, name="w1_sb")
-        nc.scalar.dma_start(w1_sb[:], w1)
+        nc.gpsimd.dma_start(w1_sb[:], w1)
         b1_sb = held.tile([128, ROWS_PER_PART], F32, name="b1_sb")
         nc.gpsimd.dma_start(b1_sb[:], b1.rearrange("(p r) o -> p (r o)", p=128))
 
@@ -44,27 +46,35 @@ def tile_canonicalgraphadapter_kernel(tc, x, pw, lab_bias, w1, b1, offs, out):
         warmed = held.tile([128, 1], F32, name="warmed")
         nc.scalar.activation(warmed[:], zero[:], IDENTITY)
 
-        pick = [held.tile([PAIRS, FEAT], BF16, name=f"pick{i}") for i in range(PAIRS)]
+        take = held.tile([COPIES * PAIRS, 1], F32, name="take")
+        nc.vector.memset(take[:], -1.0)
+        nc.vector.memset(take[0:PAIRS, :], 0.0)
+        pick = held.tile([COPIES * PAIRS, PAIRS], BF16, name="pick")
+        nc.vector.memset(pick[:], 0.0)
         for i in range(PAIRS):
-            nc.vector.memset(pick[i][:], 0.0)
-            nc.vector.memset(pick[i][0 : i + 1, :], 1.0)
-            if i > 0:
-                nc.vector.memset(pick[i][0:i, :], 0.0)
+            for k in reversed(range(COPIES)):
+                row = PAIRS * k + i
+                nc.vector.memset(pick[0 : row + 1, i : i + 1], 1.0)
+                if row > 0:
+                    nc.vector.memset(pick[0:row, i : i + 1], 0.0)
 
         def upper(tile):
             return tile[:].bitcast(BF16).rearrange("i (j two) -> i j two", two=2)[:, :, 1]
 
-        parts = [pw_rows] + [held.tile([PAIRS, SAMPLES], F32, name=f"rest{k}") for k in range(2)]
-        for k in range(2):
-            nc.vector.tensor_tensor(parts[k + 1][:], parts[k][:], upper(parts[k]), SUBTRACT)
+        rest = held.tile([COPIES * PAIRS, SAMPLES], F32, name="rest")
+        nc.vector.tensor_tensor(rest[:], pw_rows[:], upper(pw_rows), SUBTRACT)
+        later = held.tile([COPIES * PAIRS, SAMPLES], F32, name="later")
+        nc.vector.scalar_tensor_tensor(later[:], upper(rest), take[:, 0:1], rest[:], MULT, ADD)
         pw_all = [
             [psum.tile([FEAT, SAMPLES], F32, name=f"pw_all{e}_{a}") for a in range(NODES)] for e in range(NODES)
         ]
-        for e in range(NODES):
-            for k in range(3):
+        for rows, source in ((PAIRS, pw_rows), (COPIES * PAIRS, later)):
+            for e in range(NODES):
                 for a in range(NODES):
+                    i = 2 * a + e
                     nc.tensor.matmul(
-                        pw_all[e][a][:], pick[2 * a + e][:], upper(parts[k]), start=k == 0, stop=k == 2
+                        pw_all[e][a][:], pick[0:rows, i : i + 1].to_broadcast([rows, FEAT]), upper(source)[0:rows],
+                        start=source is pw_rows, stop=source is later,
                     )
 
         prod = [held.tile([FEAT, NODES, SAMPLES], F32, name=f"prod{e}") for e in range(NODES)]

@@ -30,14 +30,14 @@ def tile_canonicalgraphadapter_kernel(tc, x, pw, lab_bias, w1, b1, offs, out):
         nc.sync.dma_start(pw_rows[0:PAIRS, :], pw.rearrange("a e j -> (a e) j"))
         nc.scalar.dma_start(pw_rows[PAIRS : COPIES * PAIRS, :], pw.rearrange("a e j -> (a e) j"))
         x_sb = held.tile([FEAT, NODES, SAMPLES], F32, name="x_sb")
-        nc.scalar.dma_start(x_sb[:], x.rearrange("(a f) j -> f a j", f=FEAT))
+        nc.sync.dma_start(x_sb[:], x.rearrange("(a f) j -> f a j", f=FEAT))
         offsets = held.tile([128, SAMPLES // 16], U16, name="offsets")
         nc.sync.dma_start(offsets[:], offs)
         lab_sb = [held.tile([FEAT, LABS], F32, name=f"lab_sb{e}") for e in range(NODES)]
         nc.scalar.dma_start(lab_sb[0][:], lab_bias[0:FEAT, :])
-        nc.sync.dma_start(lab_sb[1][:], lab_bias[FEAT : 2 * FEAT, :])
+        nc.gpsimd.dma_start(lab_sb[1][:], lab_bias[FEAT : 2 * FEAT, :])
         w1_sb = held.tile([FEAT, HIDDEN], BF16, name="w1_sb")
-        nc.gpsimd.dma_start(w1_sb[:], w1)
+        nc.scalar.dma_start(w1_sb[:], w1)
         b1_sb = held.tile([128, ROWS_PER_PART], F32, name="b1_sb")
         nc.gpsimd.dma_start(b1_sb[:], b1.rearrange("(p r) o -> p (r o)", p=128))
 

import concourse.mybir as mybir

F32 = mybir.dt.float32
BF16 = mybir.dt.bfloat16
U16 = mybir.dt.uint16
MULT = mybir.AluOpType.mult
ADD = mybir.AluOpType.add
SUBTRACT = mybir.AluOpType.subtract
IDENTITY = mybir.ActivationFunctionType.Identity

NODES = 2
FEAT = 128
HIDDEN = 256
LABS = 256
SAMPLES = 128
PAIRS = NODES * NODES
COPIES = 2
ROWS_PER_PART = HIDDEN // 128

FLOPS = 2 * NODES * FEAT * HIDDEN * SAMPLES


def tile_canonicalgraphadapter_kernel(tc, x, pw, lab_bias, w1, b1, offs, out):
    nc = tc.nc
    with (
        tc.tile_pool(name="held", bufs=1) as held,
        tc.psum_pool(name="psum", bufs=1) as psum,
    ):
        pw_rows = held.tile([COPIES * PAIRS, SAMPLES], F32, name="pw_rows")
        nc.sync.dma_start(pw_rows[0:PAIRS, :], pw.rearrange("a e j -> (a e) j"))
        nc.scalar.dma_start(pw_rows[PAIRS : COPIES * PAIRS, :], pw.rearrange("a e j -> (a e) j"))
        x_sb = held.tile([FEAT, NODES, SAMPLES], F32, name="x_sb")
        nc.sync.dma_start(x_sb[:], x.rearrange("(a f) j -> f a j", f=FEAT))
        offsets = held.tile([128, SAMPLES // 16], U16, name="offsets")
        nc.sync.dma_start(offsets[:], offs)
        lab_sb = [held.tile([FEAT, LABS], F32, name=f"lab_sb{e}") for e in range(NODES)]
        nc.scalar.dma_start(lab_sb[0][:], lab_bias[0:FEAT, :])
        nc.gpsimd.dma_start(lab_sb[1][:], lab_bias[FEAT : 2 * FEAT, :])
        w1_sb = held.tile([FEAT, HIDDEN], BF16, name="w1_sb")
        nc.scalar.dma_start(w1_sb[:], w1)
        b1_sb = held.tile([128, ROWS_PER_PART], F32, name="b1_sb")
        nc.gpsimd.dma_start(b1_sb[:], b1.rearrange("(p r) o -> p (r o)", p=128))

        zero = held.tile([128, 1], F32, name="zero")
        nc.vector.memset(zero[:], 0.0)
        warmed = held.tile([128, 1], F32, name="warmed")
        nc.scalar.activation(warmed[:], zero[:], IDENTITY)

        take = held.tile([COPIES * PAIRS, 1], F32, name="take")
        nc.vector.memset(take[:], -1.0)
        nc.vector.memset(take[0:PAIRS, :], 0.0)
        pick = held.tile([COPIES * PAIRS, PAIRS], BF16, name="pick")
        nc.vector.memset(pick[:], 0.0)
        for i in range(PAIRS):
            for k in reversed(range(COPIES)):
                row = PAIRS * k + i
                nc.vector.memset(pick[0 : row + 1, i : i + 1], 1.0)
                if row > 0:
                    nc.vector.memset(pick[0:row, i : i + 1], 0.0)

        def upper(tile):
            return tile[:].bitcast(BF16).rearrange("i (j two) -> i j two", two=2)[:, :, 1]

        rest = held.tile([COPIES * PAIRS, SAMPLES], F32, name="rest")
        nc.vector.tensor_tensor(rest[:], pw_rows[:], upper(pw_rows), SUBTRACT)
        later = held.tile([COPIES * PAIRS, SAMPLES], F32, name="later")
        nc.vector.scalar_tensor_tensor(later[:], upper(rest), take[:, 0:1], rest[:], MULT, ADD)
        pw_all = [
            [psum.tile([FEAT, SAMPLES], F32, name=f"pw_all{e}_{a}") for a in range(NODES)] for e in range(NODES)
        ]
        for rows, source in ((PAIRS, pw_rows), (COPIES * PAIRS, later)):
            for e in range(NODES):
                for a in range(NODES):
                    i = 2 * a + e
                    nc.tensor.matmul(
                        pw_all[e][a][:], pick[0:rows, i : i + 1].to_broadcast([rows, FEAT]), upper(source)[0:rows],
                        start=source is pw_rows, stop=source is later,
                    )

        prod = [held.tile([FEAT, NODES, SAMPLES], F32, name=f"prod{e}") for e in range(NODES)]
        mix = [held.tile([FEAT, SAMPLES], F32, name=f"mix{e}") for e in range(NODES)]
        y32 = [held.tile([FEAT, SAMPLES], F32, name=f"y32_{e}") for e in range(NODES)]
        y_bf = [held.tile([FEAT, SAMPLES], BF16, name=f"y_bf{e}") for e in range(NODES)]

        def product(e):
            for a in range(NODES):
                nc.vector.tensor_tensor(prod[e][:, a, :], x_sb[:, a, :], pw_all[e][a][:], MULT)

        def total(e):
            nc.vector.tensor_tensor(mix[e][:], prod[e][:, 0, :], prod[e][:, 1, :], ADD)

        def look_up_and_add(e):
            nc.vector.tensor_tensor(y32[e][:], lab_sb[e][:].indirect(offsets[:]), mix[e][:], ADD)

        def round_to_bf16(e):
            nc.vector.tensor_copy(y_bf[e][:], y32[e][:])

        for e in range(NODES):
            product(e)
            total(e)
            look_up_and_add(e)
            round_to_bf16(e)

        w1_by_r = w1_sb[:].rearrange("f (p r) -> f r p", r=ROWS_PER_PART)
        out_by_node = out.rearrange("(e p r) j -> e p (r j)", e=NODES, r=ROWS_PER_PART)
        for e in range(NODES):
            res = held.tile([128, ROWS_PER_PART, SAMPLES], F32, name=f"res{e}")
            acc = [psum.tile([128, SAMPLES], F32, name=f"acc{e}_{r}") for r in range(ROWS_PER_PART)]
            for r in reversed(range(ROWS_PER_PART)):
                nc.tensor.matmul(acc[r][:], w1_by_r[:, r, :], y_bf[e][:], start=True, stop=True)
            nc.vector.tensor_scalar(res[:, 0, :], acc[0][:], b1_sb[:, 0:1], None, ADD)
            nc.scalar.activation(res[:, 1, :], acc[1][:], IDENTITY, bias=b1_sb[:, 1:2])
            nc.sync.dma_start(out_by_node[e], res[:].rearrange("p r j -> p (r j)"))
